import numpy as np
import ml_dtypes


def mxq(x, axis, fmt="e4m3"):
    dtype, down = {"e4m3": (ml_dtypes.float8_e4m3fn, 7), "e5m2": (ml_dtypes.float8_e5m2, 14)}[fmt]
    v = np.moveaxis(np.asarray(x, np.float32).astype(ml_dtypes.bfloat16).astype(np.float64), axis, -1)
    blocks = v.reshape(v.shape[:-1] + (-1, 32))
    amax = np.abs(blocks).max(-1, keepdims=True)
    byte = np.maximum(np.where(amax > 0, np.frexp(amax)[1] - 1 + 127, 0) - down, 1)
    scale = np.exp2(byte - 127.0)
    codes = (blocks / scale).astype(np.float32).astype(dtype).astype(np.float64)
    return np.moveaxis((codes * scale).reshape(v.shape), -1, axis)


WIDE = False


def mx_kscale(k):
    if not WIDE:
        return np.ones(k)
    levels = np.array([10, -10, 5, -5, 0])
    a = np.random.permutation(np.resize(levels, k // 512 * 4)).reshape(k // 512, 4)
    idx = np.arange(k)
    return np.exp2(a[idx // 512, idx % 128 // 32])


BF16 = ml_dtypes.bfloat16


def bf(x):
    return np.asarray(x, np.float32).astype(BF16)


def f64(x):
    return np.asarray(x).astype(np.float64)


E2M1 = np.array([0.0, 0.5, 1.0, 1.5, 2.0, 3.0, 4.0, 6.0, -0.0, -0.5, -1.0, -1.5, -2.0, -3.0, -4.0, -6.0])


def pack_weight(w, fmt):
    k, n = w.shape
    w = f64(bf(w)).reshape(k // 32, 32, n)
    amax = np.abs(w).max(1)
    if fmt == "e4m3":
        byte = np.frexp(amax)[1] - 1 + 127 - 7
    else:
        mant, ex = np.frexp(amax / 6.0)
        byte = np.where(mant > 0.5, ex, ex - 1) + 127
    byte = np.clip(np.where(amax > 0, byte, 1), 1, 254)
    scaled = (w * np.exp2(127.0 - byte)[:, None, :]).reshape(k, n).astype(np.float32)
    by_word = np.ascontiguousarray(scaled.reshape(k // 512, 128, 4, n).transpose(0, 1, 3, 2))
    if fmt == "e4m3":
        words = by_word.astype(ml_dtypes.float8_e4m3fn).view(np.uint8)
    else:
        c = by_word.astype(ml_dtypes.float4_e2m1fn).view(np.uint8) & 0xF
        words = c[..., 0::2] | (c[..., 1::2] << 4)
    return np.ascontiguousarray(words), np.ascontiguousarray(byte.astype(np.uint8).reshape(k // 512, 16, n))


def unpack_weight(words, scales, fmt):
    g, p, n, _ = words.shape
    if fmt == "e4m3":
        vals = np.ascontiguousarray(words).view(ml_dtypes.float8_e4m3fn).astype(np.float64)
    else:
        nib = np.empty((g, p, n, 4), np.uint8)
        nib[..., 0::2] = words & 0xF
        nib[..., 1::2] = words >> 4
        vals = E2M1[nib]
    vals = vals * np.repeat(np.exp2(scales.astype(np.float64) - 127.0), 8, axis=1)[..., None]
    return vals.transpose(0, 1, 3, 2).reshape(g * 512, n)

def pack4(w):
    words, scales = pack_weight(w, "e2m1")
    return words.reshape(words.shape[0], 128, -1), scales


def unpack4(words, scales):
    return unpack_weight(words.reshape(words.shape[0], 128, -1, 2), scales, "e2m1")


B, C, H, W, S = 2, 512, 128, 64, 4
NB = (H // S) * (W // S)


def setup_inputs():
    s = mx_kscale(C)
    x = bf(np.random.standard_normal((B, C, H, W)) * s[None, :, None, None])
    wq = np.random.standard_normal((C, C)) * 1.2 * S / np.sqrt(C) / s[None, :]
    Wq_words, Wq_scales = pack4(np.ascontiguousarray(wq.T))
    bq = bf(np.random.standard_normal(C) * 0.3)
    wk = np.random.standard_normal((C, C)) * 1.2 * S / np.sqrt(C) / s[None, :]
    Wk_words, Wk_scales = pack4(np.ascontiguousarray(wk.T))
    bk = bf(np.random.standard_normal(C) * 0.3)
    return {"x": x,
            "Wq_words": Wq_words, "Wq_scales": Wq_scales,
            "bq": bq,
            "Wk_words": Wk_words, "Wk_scales": Wk_scales,
            "bk": bk}


def reference(x, Wq_words, Wq_scales, bq, Wk_words, Wk_scales, bk):
    x_avg = f64(x).reshape(B, C, H // S, S, W // S, S).mean(axis=(3, 5))
    x_avg = x_avg.reshape(B, C, NB).transpose(0, 2, 1)
    xq = mxq(x_avg, 2, "e4m3")
    Q = (xq @ unpack4(Wq_words, Wq_scales)) + f64(bq)
    K = (xq @ unpack4(Wk_words, Wk_scales)) + f64(bk)
    return Q, K

@@ -1,0 +1,128 @@
+import concourse.mybir as mybir
+
+BF16 = mybir.dt.bfloat16
+F32 = mybir.dt.float32
+I32 = mybir.dt.int32
+U8 = mybir.dt.uint8
+U32 = mybir.dt.uint32
+FP8X4 = mybir.dt.float8_e4m3fn_x4
+FP4X4 = mybir.dt.float4_e2m1fn_x4
+ADD = mybir.AluOpType.add
+
+B, C, H, W, S = 2, 512, 128, 64, 4
+P = 128
+PACK = 4
+BLOCK_COLS = W // S
+STRIP = S * W
+STRIPS = P // BLOCK_COLS
+CHUNK = STRIPS * STRIP
+CHUNKS = H * W // CHUNK
+
+VECTOR_STRIPS = 5
+GPSIMD_STRIPS = STRIPS - VECTOR_STRIPS
+
+FLOPS = 2 * 2 * B * (H // S) * (W // S) * C * C
+
+
+def pool_on_vector(nc, x_chunk, sums):
+    blocks = VECTOR_STRIPS * BLOCK_COLS
+    for t in range(PACK):
+        pixels = x_chunk[:, t, : VECTOR_STRIPS * STRIP].rearrange(
+            "p (r i c j) -> p r c i j", i=S, c=BLOCK_COLS, j=S
+        )
+        nc.vector.tensor_reduce(
+            out=sums[:, t, :blocks].rearrange("p (r c) -> p r c", c=BLOCK_COLS),
+            in_=pixels,
+            axis=mybir.AxisListType.XY,
+            op=ADD,
+        )
+
+
+def pool_on_gpsimd(nc, work, x_chunk, sums):
+    first = VECTOR_STRIPS * STRIP
+    rows = x_chunk[:, :, first:].rearrange("p t (a i w) -> p t a i w", i=2, w=W)
+    row_pairs = work.tile([P, PACK, 2 * GPSIMD_STRIPS, W], F32)
+    nc.gpsimd.tensor_tensor(out=row_pairs[:], in0=rows[:, :, :, 0, :], in1=rows[:, :, :, 1, :], op=ADD)
+    halves = row_pairs[:].rearrange("p t (r h) w -> p (t r) h w", h=2)
+    columns = work.tile([P, PACK * GPSIMD_STRIPS, W], F32)
+    nc.gpsimd.tensor_tensor(out=columns[:], in0=halves[:, :, 0, :], in1=halves[:, :, 1, :], op=ADD)
+    pairs = columns[:].rearrange("p a (c e) -> p (a c) e", e=2)
+    column_pairs = work.tile([P, PACK * GPSIMD_STRIPS * W // 2], F32)
+    nc.gpsimd.tensor_tensor(out=column_pairs[:], in0=pairs[:, :, 0], in1=pairs[:, :, 1], op=ADD)
+    quads = column_pairs[:].rearrange("p (t n e) -> p t n e", t=PACK, e=2)
+    nc.gpsimd.tensor_tensor(
+        out=sums[:, :, VECTOR_STRIPS * BLOCK_COLS :], in0=quads[:, :, :, 0], in1=quads[:, :, :, 1], op=ADD
+    )
+
+
+def tile_coarseblockattention_pa_kernel(
+    tc, x, Wq_words, Wq_scales, bq, Wk_words, Wk_scales, bk, out_0, out_1
+):
+    nc = tc.nc
+    projections = ((Wq_words, Wq_scales, bq, out_0), (Wk_words, Wk_scales, bk, out_1))
+
+    with tc.tile_pool(name="keep", bufs=1) as keep, tc.tile_pool(
+        name="image", bufs=B * CHUNKS
+    ) as image, tc.tile_pool(name="work", bufs=2) as work, tc.tile_pool(
+        name="results", bufs=3
+    ) as results, tc.psum_pool(name="psum", bufs=2) as psum:
+        w_words = keep.tile([P, 2, 2 * C], U8, align_bytes=64)
+        w_scales = keep.tile([P, 2, C], U8, align_bytes=64)
+        bias = keep.tile([P, 2, C], BF16)
+        nc.vector.memset(w_scales[:].rearrange("p w n -> p (w n)").bitcast(I32), 0)
+
+        x_chunks = []
+        for b in range(B):
+            channels = x[b].rearrange("(p t) h w -> p t (h w)", t=PACK)
+            for m in range(CHUNKS):
+                x_chunk = image.tile([P, PACK, CHUNK], BF16)
+                nc.sync.dma_start(out=x_chunk[:], in_=channels[:, :, m * CHUNK : (m + 1) * CHUNK])
+                x_chunks.append(x_chunk)
+                if b == 0 and m == 0:
+                    for w in range(2):
+                        words, scales, b_vec, out = projections[w]
+                        nc.sync.dma_start(out=w_words[:, w, :].bitcast(I32), in_=words[0].bitcast(I32))
+                        for quadrant in range(4):
+                            nc.sync.dma_start(
+                                out=w_scales[32 * quadrant : 32 * quadrant + 4, w, :].bitcast(I32),
+                                in_=scales[0, 4 * quadrant : 4 * quadrant + 4, :].bitcast(I32),
+                            )
+                        nc.sync.dma_start(out=bias[:, w, :], in_=b_vec.partition_broadcast(P))
+
+        for b in range(B):
+            for m in range(CHUNKS):
+                x_chunk = x_chunks[b * CHUNKS + m]
+                sums = work.tile([P, PACK, P], F32)
+                pool_on_vector(nc, x_chunk, sums)
+                pool_on_gpsimd(nc, work, x_chunk, sums)
+
+                grouped = work.tile([P, P, PACK], BF16, align_bytes=64)
+                nc.scalar.activation(
+                    out=grouped[:],
+                    in_=sums[:].rearrange("p t n -> p n t"),
+                    func=mybir.ActivationFunctionType.Copy,
+                    scale=1.0 / (S * S),
+                )
+                x_codes = work.tile([P, P], U32, align_bytes=64)
+                x_scales = work.tile([P, P], U8, align_bytes=64)
+                nc.vector.quantize_mx(
+                    out=x_codes[:].bitcast(FP8X4),
+                    scales=x_scales[:],
+                    in_=grouped[:].rearrange("p n t -> p (n t)"),
+                )
+
+                result = results.tile([P, 2, C], F32)
+                for w in range(2):
+                    words, scales, b_vec, out = projections[w]
+                    acc = psum.tile([P, C], F32, name="acc%d" % w)
+                    nc.tensor.matmul_mx(
+                        out=acc[:],
+                        lhsT=x_codes[:].bitcast(FP8X4),
+                        lhsT_scale=x_scales[:],
+                        rhs=w_words[:, w, :].bitcast(FP4X4),
+                        rhs_scale=w_scales[:, w, :],
+                        start=True,
+                        stop=True,
+                    )
+                    nc.vector.tensor_tensor(out=result[:, w, :], in0=acc[:], in1=bias[:, w, :], op=ADD)
+                    nc.sync.dma_start(out=out[b, m * P : (m + 1) * P, :], in_=result[:, w, :])

@@ -1,4 +1,5 @@
 import concourse.mybir as mybir
+from concourse.masks import make_identity
 
 BF16 = mybir.dt.bfloat16
 F32 = mybir.dt.float32
@@ -8,6 +9,7 @@ U32 = mybir.dt.uint32
 FP8X4 = mybir.dt.float8_e4m3fn_x4
 FP4X4 = mybir.dt.float4_e2m1fn_x4
 ADD = mybir.AluOpType.add
+COPY = mybir.ActivationFunctionType.Copy
 
 B, C, H, W, S = 2, 512, 128, 64, 4
 P = 128
@@ -18,41 +20,62 @@ STRIPS = P // BLOCK_COLS
 CHUNK = STRIPS * STRIP
 CHUNKS = H * W // CHUNK
 
-VECTOR_STRIPS = 5
-GPSIMD_STRIPS = STRIPS - VECTOR_STRIPS
+TENSOR_STRIPS = 3
+GPSIMD_STRIPS = 2
+VECTOR_STRIPS = STRIPS - TENSOR_STRIPS - GPSIMD_STRIPS
+TENSOR_BLOCKS = TENSOR_STRIPS * BLOCK_COLS
+GPSIMD_BLOCKS = GPSIMD_STRIPS * BLOCK_COLS
 
 FLOPS = 2 * 2 * B * (H // S) * (W // S) * C * C
 
 
-def pool_on_vector(nc, x_chunk, sums):
-    blocks = VECTOR_STRIPS * BLOCK_COLS
+def pool_on_tensor(nc, work, psum, x_chunk, identity, block_of_pixel, sums):
+    half_strips = 2 * TENSOR_STRIPS
     for t in range(PACK):
-        pixels = x_chunk[:, t, : VECTOR_STRIPS * STRIP].rearrange(
-            "p (r i c j) -> p r c i j", i=S, c=BLOCK_COLS, j=S
-        )
-        nc.vector.tensor_reduce(
-            out=sums[:, t, :blocks].rearrange("p (r c) -> p r c", c=BLOCK_COLS),
-            in_=pixels,
-            axis=mybir.AxisListType.XY,
-            op=ADD,
-        )
+        turned = psum.tile([P, half_strips, P], BF16)
+        for k in range(half_strips):
+            nc.tensor.transpose(turned[:, k, :], x_chunk[:, t, k * P : (k + 1) * P], identity[:])
+        pixels = work.tile([P, half_strips, P], BF16)
+        nc.scalar.copy(out=pixels[:], in_=turned[:])
+        for k in range(half_strips):
+            strip = k // 2
+            nc.tensor.matmul(
+                out=sums[:, t, strip * BLOCK_COLS : (strip + 1) * BLOCK_COLS],
+                lhsT=pixels[:, k, :],
+                rhs=block_of_pixel[:],
+                start=(k % 2 == 0),
+                stop=(k % 2 == 1),
+            )
 
 
 def pool_on_gpsimd(nc, work, x_chunk, sums):
-    first = VECTOR_STRIPS * STRIP
-    rows = x_chunk[:, :, first:].rearrange("p t (a i w) -> p t a i w", i=2, w=W)
+    first = TENSOR_STRIPS * STRIP
+    rows = x_chunk[:, :, first : first + GPSIMD_STRIPS * STRIP].rearrange(
+        "p t (a i w) -> p t a i w", i=2, w=W
+    )
     row_pairs = work.tile([P, PACK, 2 * GPSIMD_STRIPS, W], F32)
     nc.gpsimd.tensor_tensor(out=row_pairs[:], in0=rows[:, :, :, 0, :], in1=rows[:, :, :, 1, :], op=ADD)
-    halves = row_pairs[:].rearrange("p t (r h) w -> p (t r) h w", h=2)
+    upper_lower = row_pairs[:].rearrange("p t (r h) w -> p (t r) h w", h=2)
     columns = work.tile([P, PACK * GPSIMD_STRIPS, W], F32)
-    nc.gpsimd.tensor_tensor(out=columns[:], in0=halves[:, :, 0, :], in1=halves[:, :, 1, :], op=ADD)
+    nc.gpsimd.tensor_tensor(out=columns[:], in0=upper_lower[:, :, 0, :], in1=upper_lower[:, :, 1, :], op=ADD)
     pairs = columns[:].rearrange("p a (c e) -> p (a c) e", e=2)
     column_pairs = work.tile([P, PACK * GPSIMD_STRIPS * W // 2], F32)
     nc.gpsimd.tensor_tensor(out=column_pairs[:], in0=pairs[:, :, 0], in1=pairs[:, :, 1], op=ADD)
     quads = column_pairs[:].rearrange("p (t n e) -> p t n e", t=PACK, e=2)
     nc.gpsimd.tensor_tensor(
-        out=sums[:, :, VECTOR_STRIPS * BLOCK_COLS :], in0=quads[:, :, :, 0], in1=quads[:, :, :, 1], op=ADD
+        out=sums[:, :, :GPSIMD_BLOCKS], in0=quads[:, :, :, 0], in1=quads[:, :, :, 1], op=ADD
     )
+
+
+def pool_on_vector(nc, x_chunk, sums):
+    first = (TENSOR_STRIPS + GPSIMD_STRIPS) * STRIP
+    for t in range(PACK):
+        nc.vector.tensor_reduce(
+            out=sums[:, t, GPSIMD_BLOCKS:].rearrange("p (r c) -> p r c", c=BLOCK_COLS),
+            in_=x_chunk[:, t, first:].rearrange("p (r i c j) -> p r c i j", i=S, c=BLOCK_COLS, j=S),
+            axis=mybir.AxisListType.XY,
+            op=ADD,
+        )
 
 
 def tile_coarseblockattention_pa_kernel(
@@ -89,18 +112,38 @@ def tile_coarseblockattention_pa_kernel(
                             )
                         nc.sync.dma_start(out=bias[:, w, :], in_=b_vec.partition_broadcast(P))
 
+        identity = keep.tile([P, P], BF16)
+        make_identity(nc, identity[:])
+        membership = keep.tile([P, BLOCK_COLS], F32)
+        nc.vector.tensor_reduce(
+            out=membership[:],
+            in_=identity[:].rearrange("p (i c j) -> p c i j", i=2, c=BLOCK_COLS, j=S),
+            axis=mybir.AxisListType.XY,
+            op=ADD,
+        )
+        block_of_pixel = keep.tile([P, BLOCK_COLS], BF16)
+        nc.vector.tensor_copy(out=block_of_pixel[:], in_=membership[:])
+
         for b in range(B):
             for m in range(CHUNKS):
                 x_chunk = x_chunks[b * CHUNKS + m]
-                sums = work.tile([P, PACK, P], F32)
-                pool_on_vector(nc, x_chunk, sums)
-                pool_on_gpsimd(nc, work, x_chunk, sums)
+                tensor_sums = psum.tile([P, PACK, TENSOR_BLOCKS], F32)
+                other_sums = work.tile([P, PACK, P - TENSOR_BLOCKS], F32)
+                pool_on_tensor(nc, work, psum, x_chunk, identity, block_of_pixel, tensor_sums)
+                pool_on_gpsimd(nc, work, x_chunk, other_sums)
+                pool_on_vector(nc, x_chunk, other_sums)
 
                 grouped = work.tile([P, P, PACK], BF16, align_bytes=64)
                 nc.scalar.activation(
-                    out=grouped[:],
-                    in_=sums[:].rearrange("p t n -> p n t"),
-                    func=mybir.ActivationFunctionType.Copy,
+                    out=grouped[:, :TENSOR_BLOCKS, :],
+                    in_=tensor_sums[:].rearrange("p t n -> p n t"),
+                    func=COPY,
+                    scale=1.0 / (S * S),
+                )
+                nc.scalar.activation(
+                    out=grouped[:, TENSOR_BLOCKS:, :],
+                    in_=other_sums[:].rearrange("p t n -> p n t"),
+                    func=COPY,
                     scale=1.0 / (S * S),
                 )
                 x_codes = work.tile([P, P], U32, align_bytes=64)

@@ -9,7 +9,6 @@ U32 = mybir.dt.uint32
 FP8X4 = mybir.dt.float8_e4m3fn_x4
 FP4X4 = mybir.dt.float4_e2m1fn_x4
 ADD = mybir.AluOpType.add
-COPY = mybir.ActivationFunctionType.Copy
 
 B, C, H, W, S = 2, 512, 128, 64, 4
 P = 128
@@ -19,101 +18,143 @@ STRIP = S * W
 STRIPS = P // BLOCK_COLS
 CHUNK = STRIPS * STRIP
 CHUNKS = H * W // CHUNK
+N_CHUNKS = B * CHUNKS
 
 TENSOR_STRIPS = 3
 GPSIMD_STRIPS = 2
 VECTOR_STRIPS = STRIPS - TENSOR_STRIPS - GPSIMD_STRIPS
 TENSOR_BLOCKS = TENSOR_STRIPS * BLOCK_COLS
-GPSIMD_BLOCKS = GPSIMD_STRIPS * BLOCK_COLS
+VECTOR_BLOCK = TENSOR_BLOCKS + GPSIMD_STRIPS * BLOCK_COLS
+GPSIMD_FIRST = TENSOR_STRIPS * STRIP
+VECTOR_FIRST = GPSIMD_FIRST + GPSIMD_STRIPS * STRIP
+
+SPLIT_CHUNKS = 3
 
 FLOPS = 2 * 2 * B * (H // S) * (W // S) * C * C
 
 
+def spread_biases(nc, keep, psum, identity, bq, bk):
+    pieces = 2 * C // P
+    bias_rows = keep.tile([P, P], BF16)
+    nc.vector.memset(bias_rows[:].bitcast(I32), 0)
+    nc.sync.dma_start(out=bias_rows[: pieces // 2, :], in_=bq.rearrange("(j k) -> j k", k=P))
+    nc.sync.dma_start(out=bias_rows[pieces // 2 : pieces, :], in_=bk.rearrange("(j k) -> j k", k=P))
+    turned_rows = psum.tile([P, P], BF16, tag="turned")
+    nc.tensor.transpose(turned_rows[:], bias_rows[:], identity[:])
+    bias_columns = keep.tile([P, pieces], BF16)
+    nc.scalar.copy(out=bias_columns[:], in_=turned_rows[:, :pieces])
+    spread = psum.tile([P, pieces, P], BF16, tag="turned")
+    for j in range(pieces):
+        nc.tensor.transpose(spread[:, j, :], bias_columns[:, j : j + 1].to_broadcast([P, P]), identity[:])
+    bias = keep.tile([P, 2, C], BF16)
+    nc.scalar.copy(out=bias[:].rearrange("p w (j k) -> p (w j) k", k=P), in_=spread[:])
+    return bias
+
+
 def pool_on_tensor(nc, work, psum, x_chunk, identity, block_of_pixel, sums):
     half_strips = 2 * TENSOR_STRIPS
-    for t in range(PACK):
-        turned = psum.tile([P, half_strips, P], BF16)
-        for k in range(half_strips):
-            nc.tensor.transpose(turned[:, k, :], x_chunk[:, t, k * P : (k + 1) * P], identity[:])
-        pixels = work.tile([P, half_strips, P], BF16)
-        nc.scalar.copy(out=pixels[:], in_=turned[:])
-        for k in range(half_strips):
-            strip = k // 2
-            nc.tensor.matmul(
-                out=sums[:, t, strip * BLOCK_COLS : (strip + 1) * BLOCK_COLS],
-                lhsT=pixels[:, k, :],
-                rhs=block_of_pixel[:],
-                start=(k % 2 == 0),
-                stop=(k % 2 == 1),
-            )
+    tensor_sums = psum.tile([P, PACK, TENSOR_BLOCKS], F32)
+    copies = []
+    for t in range(PACK + 1):
+        if t < PACK:
+            turned = psum.tile([P, half_strips, P], BF16)
+            for k in range(half_strips):
+                nc.tensor.transpose(turned[:, k, :], x_chunk[:, t, k * P : (k + 1) * P], identity[:])
+            pixels = work.tile([P, half_strips, P], BF16)
+            nc.scalar.copy(out=pixels[:], in_=turned[:])
+            copies.append(pixels)
+        if t > 0:
+            for k in range(half_strips):
+                strip = k // 2
+                nc.tensor.matmul(
+                    out=tensor_sums[:, t - 1, strip * BLOCK_COLS : (strip + 1) * BLOCK_COLS],
+                    lhsT=copies[t - 1][:, k, :],
+                    rhs=block_of_pixel[:],
+                    start=(k % 2 == 0),
+                    stop=(k % 2 == 1),
+                )
+    nc.scalar.copy(out=sums[:, :TENSOR_BLOCKS, :], in_=tensor_sums[:].rearrange("p t n -> p n t"))
 
 
 def pool_on_gpsimd(nc, work, x_chunk, sums):
-    first = TENSOR_STRIPS * STRIP
-    rows = x_chunk[:, :, first : first + GPSIMD_STRIPS * STRIP].rearrange(
-        "p t (a i w) -> p t a i w", i=2, w=W
-    )
+    rows = x_chunk[:, :, GPSIMD_FIRST:VECTOR_FIRST].rearrange("p t (a i w) -> p t a i w", i=2, w=W)
     row_pairs = work.tile([P, PACK, 2 * GPSIMD_STRIPS, W], F32)
     nc.gpsimd.tensor_tensor(out=row_pairs[:], in0=rows[:, :, :, 0, :], in1=rows[:, :, :, 1, :], op=ADD)
     upper_lower = row_pairs[:].rearrange("p t (r h) w -> p (t r) h w", h=2)
     columns = work.tile([P, PACK * GPSIMD_STRIPS, W], F32)
-    nc.gpsimd.tensor_tensor(out=columns[:], in0=upper_lower[:, :, 0, :], in1=upper_lower[:, :, 1, :], op=ADD)
+    nc.gpsimd.tensor_tensor(
+        out=columns[:], in0=upper_lower[:, :, 0, :], in1=upper_lower[:, :, 1, :], op=ADD
+    )
     pairs = columns[:].rearrange("p a (c e) -> p (a c) e", e=2)
     column_pairs = work.tile([P, PACK * GPSIMD_STRIPS * W // 2], F32)
     nc.gpsimd.tensor_tensor(out=column_pairs[:], in0=pairs[:, :, 0], in1=pairs[:, :, 1], op=ADD)
     quads = column_pairs[:].rearrange("p (t n e) -> p t n e", t=PACK, e=2)
     nc.gpsimd.tensor_tensor(
-        out=sums[:, :, :GPSIMD_BLOCKS], in0=quads[:, :, :, 0], in1=quads[:, :, :, 1], op=ADD
+        out=sums[:, TENSOR_BLOCKS:VECTOR_BLOCK, :].rearrange("p n t -> p t n"),
+        in0=quads[:, :, :, 0],
+        in1=quads[:, :, :, 1],
+        op=ADD,
     )
 
 
 def pool_on_vector(nc, x_chunk, sums):
-    first = (TENSOR_STRIPS + GPSIMD_STRIPS) * STRIP
-    for t in range(PACK):
-        nc.vector.tensor_reduce(
-            out=sums[:, t, GPSIMD_BLOCKS:].rearrange("p (r c) -> p r c", c=BLOCK_COLS),
-            in_=x_chunk[:, t, first:].rearrange("p (r i c j) -> p r c i j", i=S, c=BLOCK_COLS, j=S),
-            axis=mybir.AxisListType.XY,
-            op=ADD,
-        )
+    with nc.allow_low_precision(reason="added up in float32; the output is the one rounding to bfloat16"):
+        for t in range(PACK):
+            nc.vector.tensor_reduce(
+                out=sums[:, VECTOR_BLOCK:, t].rearrange("p (r c) -> p r c", c=BLOCK_COLS),
+                in_=x_chunk[:, t, VECTOR_FIRST:].rearrange(
+                    "p (r i c j) -> p r c i j", i=S, c=BLOCK_COLS, j=S
+                ),
+                axis=mybir.AxisListType.XY,
+                op=ADD,
+            )
 
 
 def tile_coarseblockattention_pa_kernel(
     tc, x, Wq_words, Wq_scales, bq, Wk_words, Wk_scales, bk, out_0, out_1
 ):
     nc = tc.nc
-    projections = ((Wq_words, Wq_scales, bq, out_0), (Wk_words, Wk_scales, bk, out_1))
+    outs = (out_0, out_1)
 
     with tc.tile_pool(name="keep", bufs=1) as keep, tc.tile_pool(
-        name="image", bufs=B * CHUNKS
-    ) as image, tc.tile_pool(name="work", bufs=2) as work, tc.tile_pool(
-        name="results", bufs=3
-    ) as results, tc.psum_pool(name="psum", bufs=2) as psum:
-        w_words = keep.tile([P, 2, 2 * C], U8, align_bytes=64)
-        w_scales = keep.tile([P, 2, C], U8, align_bytes=64)
-        bias = keep.tile([P, 2, C], BF16)
-        nc.vector.memset(w_scales[:].rearrange("p w n -> p (w n)").bitcast(I32), 0)
+        name="image", bufs=N_CHUNKS
+    ) as image, tc.tile_pool(name="work", bufs=3) as work, tc.tile_pool(
+        name="results", bufs=N_CHUNKS
+    ) as results, tc.psum_pool(name="psum", bufs=2) as psum, tc.manual_schedule():
 
-        x_chunks = []
-        for b in range(B):
-            channels = x[b].rearrange("(p t) h w -> p t (h w)", t=PACK)
-            for m in range(CHUNKS):
-                x_chunk = image.tile([P, PACK, CHUNK], BF16)
-                nc.sync.dma_start(out=x_chunk[:], in_=channels[:, :, m * CHUNK : (m + 1) * CHUNK])
-                x_chunks.append(x_chunk)
-                if b == 0 and m == 0:
-                    for w in range(2):
-                        words, scales, b_vec, out = projections[w]
-                        nc.sync.dma_start(out=w_words[:, w, :].bitcast(I32), in_=words[0].bitcast(I32))
-                        for quadrant in range(4):
-                            nc.sync.dma_start(
-                                out=w_scales[32 * quadrant : 32 * quadrant + 4, w, :].bitcast(I32),
-                                in_=scales[0, 4 * quadrant : 4 * quadrant + 4, :].bitcast(I32),
-                            )
-                        nc.sync.dma_start(out=bias[:, w, :], in_=b_vec.partition_broadcast(P))
+        def load_scales(w, scales):
+            for quadrant in range(4):
+                nc.sync.dma_start(
+                    out=w_scales[32 * quadrant : 32 * quadrant + 4, w, :].bitcast(I32),
+                    in_=scales[0, 4 * quadrant : 4 * quadrant + 4, :].bitcast(I32),
+                )
+
+        def load_pixels(c, first, last):
+            channels = x[c // CHUNKS].rearrange("(p t) h w -> p t (h w)", t=PACK)
+            start = (c % CHUNKS) * CHUNK
+            nc.sync.dma_start(out=x_chunks[c][:, :, first:last], in_=channels[:, :, start + first : start + last])
 
         identity = keep.tile([P, P], BF16)
         make_identity(nc, identity[:])
+        w_words = keep.tile([P, 2, 2 * C], U8, align_bytes=64)
+        w_scales = keep.tile([P, 2, C], U8, align_bytes=64)
+        nc.vector.memset(w_scales[:].rearrange("p w n -> p (w n)").bitcast(I32), 0)
+        x_chunks = [image.tile([P, PACK, CHUNK], BF16, name="x_chunk") for c in range(N_CHUNKS)]
+
+        bias = spread_biases(nc, keep, psum, identity, bq, bk)
+        load_scales(0, Wq_scales)
+        for c in range(N_CHUNKS):
+            if c < SPLIT_CHUNKS:
+                load_pixels(c, GPSIMD_FIRST, VECTOR_FIRST)
+                load_pixels(c, VECTOR_FIRST, CHUNK)
+                load_pixels(c, 0, GPSIMD_FIRST)
+            else:
+                load_pixels(c, 0, CHUNK)
+            if c == 1:
+                load_scales(1, Wk_scales)
+                nc.sync.dma_start(out=w_words[:, 0, :].bitcast(I32), in_=Wq_words[0].bitcast(I32))
+                nc.sync.dma_start(out=w_words[:, 1, :].bitcast(I32), in_=Wk_words[0].bitcast(I32))
+
         membership = keep.tile([P, BLOCK_COLS], F32)
         nc.vector.tensor_reduce(
             out=membership[:],
@@ -124,48 +165,50 @@ def tile_coarseblockattention_pa_kernel(
         block_of_pixel = keep.tile([P, BLOCK_COLS], BF16)
         nc.vector.tensor_copy(out=block_of_pixel[:], in_=membership[:])
 
-        for b in range(B):
-            for m in range(CHUNKS):
-                x_chunk = x_chunks[b * CHUNKS + m]
-                tensor_sums = psum.tile([P, PACK, TENSOR_BLOCKS], F32)
-                other_sums = work.tile([P, PACK, P - TENSOR_BLOCKS], F32)
-                pool_on_tensor(nc, work, psum, x_chunk, identity, block_of_pixel, tensor_sums)
-                pool_on_gpsimd(nc, work, x_chunk, other_sums)
-                pool_on_vector(nc, x_chunk, other_sums)
+        sums, means, accs = {}, {}, {}
 
-                grouped = work.tile([P, P, PACK], BF16, align_bytes=64)
-                nc.scalar.activation(
-                    out=grouped[:, :TENSOR_BLOCKS, :],
-                    in_=tensor_sums[:].rearrange("p t n -> p n t"),
-                    func=COPY,
-                    scale=1.0 / (S * S),
-                )
-                nc.scalar.activation(
-                    out=grouped[:, TENSOR_BLOCKS:, :],
-                    in_=other_sums[:].rearrange("p t n -> p n t"),
-                    func=COPY,
-                    scale=1.0 / (S * S),
-                )
-                x_codes = work.tile([P, P], U32, align_bytes=64)
-                x_scales = work.tile([P, P], U8, align_bytes=64)
-                nc.vector.quantize_mx(
-                    out=x_codes[:].bitcast(FP8X4),
-                    scales=x_scales[:],
-                    in_=grouped[:].rearrange("p n t -> p (n t)"),
+        def pool(c):
+            sums[c] = work.tile([P, P, PACK], BF16, name="sums")
+            pool_on_tensor(nc, work, psum, x_chunks[c], identity, block_of_pixel, sums[c])
+            pool_on_gpsimd(nc, work, x_chunks[c], sums[c])
+            pool_on_vector(nc, x_chunks[c], sums[c])
+
+        def average(c):
+            means[c] = work.tile([P, P * PACK], BF16, name="means", align_bytes=64)
+            nc.vector.tensor_scalar_mul(
+                out=means[c][:], in0=sums[c][:].rearrange("p n t -> p (n t)"), scalar1=1.0 / (S * S)
+            )
+
+        def project(c):
+            x_codes = work.tile([P, P], U32, align_bytes=64)
+            x_scales = work.tile([P, P], U8, align_bytes=64)
+            nc.vector.quantize_mx(out=x_codes[:].bitcast(FP8X4), scales=x_scales[:], in_=means[c][:])
+            for w in range(2):
+                accs[c, w] = psum.tile([P, C], F32, name="acc%d" % w)
+                nc.tensor.matmul_mx(
+                    out=accs[c, w][:],
+                    lhsT=x_codes[:].bitcast(FP8X4),
+                    lhsT_scale=x_scales[:],
+                    rhs=w_words[:, w, :].bitcast(FP4X4),
+                    rhs_scale=w_scales[:, w, :],
+                    start=True,
+                    stop=True,
                 )
 
-                result = results.tile([P, 2, C], F32)
-                for w in range(2):
-                    words, scales, b_vec, out = projections[w]
-                    acc = psum.tile([P, C], F32, name="acc%d" % w)
-                    nc.tensor.matmul_mx(
-                        out=acc[:],
-                        lhsT=x_codes[:].bitcast(FP8X4),
-                        lhsT_scale=x_scales[:],
-                        rhs=w_words[:, w, :].bitcast(FP4X4),
-                        rhs_scale=w_scales[:, w, :],
-                        start=True,
-                        stop=True,
-                    )
-                    nc.vector.tensor_tensor(out=result[:, w, :], in0=acc[:], in1=bias[:, w, :], op=ADD)
-                    nc.sync.dma_start(out=out[b, m * P : (m + 1) * P, :], in_=result[:, w, :])
+        def finish(c):
+            result = results.tile([P, 2, C], F32)
+            first_block = (c % CHUNKS) * P
+            for w in range(2):
+                nc.vector.tensor_tensor(out=result[:, w, :], in0=accs[c, w][:], in1=bias[:, w, :], op=ADD)
+                nc.sync.dma_start(
+                    out=outs[w][c // CHUNKS, first_block : first_block + P, :], in_=result[:, w, :]
+                )
+
+        for step in range(N_CHUNKS + 2):
+            if step < N_CHUNKS:
+                pool(step)
+            if step >= 2:
+                finish(step - 2)
+            if 1 <= step <= N_CHUNKS:
+                average(step - 1)
+                project(step - 1)

@@ -20,7 +20,7 @@ CHUNK = STRIPS * STRIP
 CHUNKS = H * W // CHUNK
 N_CHUNKS = B * CHUNKS
 
-TENSOR_STRIPS = 3
+TENSOR_STRIPS = 2
 GPSIMD_STRIPS = 2
 VECTOR_STRIPS = STRIPS - TENSOR_STRIPS - GPSIMD_STRIPS
 TENSOR_BLOCKS = TENSOR_STRIPS * BLOCK_COLS

@@ -20,7 +20,7 @@ CHUNK = STRIPS * STRIP
 CHUNKS = H * W // CHUNK
 N_CHUNKS = B * CHUNKS
 
-TENSOR_STRIPS = 2
+TENSOR_STRIPS = 3
 GPSIMD_STRIPS = 2
 VECTOR_STRIPS = STRIPS - TENSOR_STRIPS - GPSIMD_STRIPS
 TENSOR_BLOCKS = TENSOR_STRIPS * BLOCK_COLS
@@ -29,6 +29,9 @@ GPSIMD_FIRST = TENSOR_STRIPS * STRIP
 VECTOR_FIRST = GPSIMD_FIRST + GPSIMD_STRIPS * STRIP
 
 SPLIT_CHUNKS = 3
+
+GROUPS = N_CHUNKS * PACK
+AHEAD = 2
 
 FLOPS = 2 * 2 * B * (H // S) * (W // S) * C * C
 
@@ -49,31 +52,6 @@ def spread_biases(nc, keep, psum, identity, bq, bk):
     bias = keep.tile([P, 2, C], BF16)
     nc.scalar.copy(out=bias[:].rearrange("p w (j k) -> p (w j) k", k=P), in_=spread[:])
     return bias
-
-
-def pool_on_tensor(nc, work, psum, x_chunk, identity, block_of_pixel, sums):
-    half_strips = 2 * TENSOR_STRIPS
-    tensor_sums = psum.tile([P, PACK, TENSOR_BLOCKS], F32)
-    copies = []
-    for t in range(PACK + 1):
-        if t < PACK:
-            turned = psum.tile([P, half_strips, P], BF16)
-            for k in range(half_strips):
-                nc.tensor.transpose(turned[:, k, :], x_chunk[:, t, k * P : (k + 1) * P], identity[:])
-            pixels = work.tile([P, half_strips, P], BF16)
-            nc.scalar.copy(out=pixels[:], in_=turned[:])
-            copies.append(pixels)
-        if t > 0:
-            for k in range(half_strips):
-                strip = k // 2
-                nc.tensor.matmul(
-                    out=tensor_sums[:, t - 1, strip * BLOCK_COLS : (strip + 1) * BLOCK_COLS],
-                    lhsT=copies[t - 1][:, k, :],
-                    rhs=block_of_pixel[:],
-                    start=(k % 2 == 0),
-                    stop=(k % 2 == 1),
-                )
-    nc.scalar.copy(out=sums[:, :TENSOR_BLOCKS, :], in_=tensor_sums[:].rearrange("p t n -> p n t"))
 
 
 def pool_on_gpsimd(nc, work, x_chunk, sums):
@@ -119,8 +97,10 @@ def tile_coarseblockattention_pa_kernel(
     with tc.tile_pool(name="keep", bufs=1) as keep, tc.tile_pool(
         name="image", bufs=N_CHUNKS
     ) as image, tc.tile_pool(name="work", bufs=3) as work, tc.tile_pool(
-        name="results", bufs=N_CHUNKS
-    ) as results, tc.psum_pool(name="psum", bufs=2) as psum, tc.manual_schedule():
+        name="flipped", bufs=AHEAD + 2
+    ) as flipped, tc.tile_pool(name="results", bufs=N_CHUNKS) as results, tc.psum_pool(
+        name="psum", bufs=2
+    ) as psum, tc.manual_schedule():
 
         def load_scales(w, scales):
             for quadrant in range(4):
@@ -136,6 +116,8 @@ def tile_coarseblockattention_pa_kernel(
 
         identity = keep.tile([P, P], BF16)
         make_identity(nc, identity[:])
+        word_identity = keep.tile([P, P], F32)
+        make_identity(nc, word_identity[:])
         w_words = keep.tile([P, 2, 2 * C], U8, align_bytes=64)
         w_scales = keep.tile([P, 2, C], U8, align_bytes=64)
         nc.vector.memset(w_scales[:].rearrange("p w n -> p (w n)").bitcast(I32), 0)
@@ -158,18 +140,49 @@ def tile_coarseblockattention_pa_kernel(
         membership = keep.tile([P, BLOCK_COLS], F32)
         nc.vector.tensor_reduce(
             out=membership[:],
-            in_=identity[:].rearrange("p (i c j) -> p c i j", i=2, c=BLOCK_COLS, j=S),
+            in_=identity[:].rearrange("p (i c j) -> p c i j", i=S, c=BLOCK_COLS, j=S // 2),
             axis=mybir.AxisListType.XY,
             op=ADD,
         )
-        block_of_pixel = keep.tile([P, BLOCK_COLS], BF16)
-        nc.vector.tensor_copy(out=block_of_pixel[:], in_=membership[:])
+        block_of_word = keep.tile([P, BLOCK_COLS], BF16)
+        nc.vector.tensor_copy(out=block_of_word[:], in_=membership[:])
+        pixels = {}
 
-        sums, means, accs = {}, {}, {}
+        def turn(g):
+            turned = psum.tile([P, TENSOR_STRIPS, P], F32)
+            for k in range(TENSOR_STRIPS):
+                strip = x_chunks[g // PACK][:, g % PACK, k * STRIP : (k + 1) * STRIP]
+                nc.tensor.transpose(turned[:, k, :], strip.bitcast(F32), word_identity[:])
+            pixels[g] = flipped.tile([P, TENSOR_STRIPS, STRIP], BF16, name="pixels")
+            nc.scalar.copy(out=pixels[g][:], in_=turned[:].bitcast(BF16))
+
+        def add_up(g, tensor_sums):
+            for k in range(TENSOR_STRIPS):
+                even_odd = pixels[g][:, k, :].rearrange("q (p e) -> q p e", e=2)
+                for e in range(2):
+                    nc.tensor.matmul(
+                        out=tensor_sums[:, g % PACK, k * BLOCK_COLS : (k + 1) * BLOCK_COLS],
+                        lhsT=even_odd[:, :, e],
+                        rhs=block_of_word[:],
+                        start=(e == 0),
+                        stop=(e == 1),
+                    )
+
+        def pool_on_tensor(c):
+            tensor_sums = psum.tile([P, PACK, TENSOR_BLOCKS], F32)
+            for g in range(c * PACK, (c + 1) * PACK):
+                if g + AHEAD < GROUPS:
+                    turn(g + AHEAD)
+                add_up(g, tensor_sums)
+            nc.scalar.copy(
+                out=sums[c][:, :TENSOR_BLOCKS, :], in_=tensor_sums[:].rearrange("p t n -> p n t")
+            )
+
+        sums, means, codes, accs, result = {}, {}, {}, {}, {}
 
         def pool(c):
             sums[c] = work.tile([P, P, PACK], BF16, name="sums")
-            pool_on_tensor(nc, work, psum, x_chunks[c], identity, block_of_pixel, sums[c])
+            pool_on_tensor(c)
             pool_on_gpsimd(nc, work, x_chunks[c], sums[c])
             pool_on_vector(nc, x_chunks[c], sums[c])
 
@@ -179,10 +192,14 @@ def tile_coarseblockattention_pa_kernel(
                 out=means[c][:], in0=sums[c][:].rearrange("p n t -> p (n t)"), scalar1=1.0 / (S * S)
             )
 
-        def project(c):
+        def quantise(c):
             x_codes = work.tile([P, P], U32, align_bytes=64)
             x_scales = work.tile([P, P], U8, align_bytes=64)
             nc.vector.quantize_mx(out=x_codes[:].bitcast(FP8X4), scales=x_scales[:], in_=means[c][:])
+            codes[c] = (x_codes, x_scales)
+
+        def multiply(c):
+            x_codes, x_scales = codes[c]
             for w in range(2):
                 accs[c, w] = psum.tile([P, C], F32, name="acc%d" % w)
                 nc.tensor.matmul_mx(
@@ -195,20 +212,27 @@ def tile_coarseblockattention_pa_kernel(
                     stop=True,
                 )
 
-        def finish(c):
-            result = results.tile([P, 2, C], F32)
+        def finish(c, w):
+            if w == 0:
+                result[c] = results.tile([P, 2, C], F32, name="result")
             first_block = (c % CHUNKS) * P
-            for w in range(2):
-                nc.vector.tensor_tensor(out=result[:, w, :], in0=accs[c, w][:], in1=bias[:, w, :], op=ADD)
-                nc.sync.dma_start(
-                    out=outs[w][c // CHUNKS, first_block : first_block + P, :], in_=result[:, w, :]
-                )
+            nc.vector.tensor_tensor(out=result[c][:, w, :], in0=accs[c, w][:], in1=bias[:, w, :], op=ADD)
+            nc.sync.dma_start(
+                out=outs[w][c // CHUNKS, first_block : first_block + P, :], in_=result[c][:, w, :]
+            )
 
+        for g in range(AHEAD):
+            turn(g)
         for step in range(N_CHUNKS + 2):
+            if step >= 2:
+                multiply(step - 2)
             if step < N_CHUNKS:
                 pool(step)
             if step >= 2:
-                finish(step - 2)
+                finish(step - 2, 0)
             if 1 <= step <= N_CHUNKS:
                 average(step - 1)
-                project(step - 1)
+            if step >= 2:
+                finish(step - 2, 1)
+            if 1 <= step <= N_CHUNKS:
+                quantise(step - 1)

@@ -20,28 +20,19 @@ CHUNK = STRIPS * STRIP
 CHUNKS = H * W // CHUNK
 N_CHUNKS = B * CHUNKS
 
-TENSOR_STRIPS = 3
-GPSIMD_STRIPS = 2
-VECTOR_STRIPS = STRIPS - TENSOR_STRIPS - GPSIMD_STRIPS
-TENSOR_BLOCKS = TENSOR_STRIPS * BLOCK_COLS
-VECTOR_BLOCK = TENSOR_BLOCKS + GPSIMD_STRIPS * BLOCK_COLS
-GPSIMD_FIRST = TENSOR_STRIPS * STRIP
-VECTOR_FIRST = GPSIMD_FIRST + GPSIMD_STRIPS * STRIP
-
-SPLIT_CHUNKS = 3
-
-GROUPS = N_CHUNKS * PACK
+GPSIMD_CHANNEL, VECTOR_CHANNEL, TENSOR_CHANNEL, SHARED_CHANNEL = 0, 1, 2, 3
+HALF = CHUNK // 2
+TENSOR_STRIPS = STRIPS + STRIPS // 2
+GROUP = 4
+GROUPS_PER_CHUNK = TENSOR_STRIPS // GROUP
+GROUPS = N_CHUNKS * GROUPS_PER_CHUNK
 AHEAD = 2
 
 FLOPS = 2 * 2 * B * (H // S) * (W // S) * C * C
 
 
-def spread_biases(nc, keep, psum, identity, bq, bk):
+def spread_biases(nc, keep, psum, identity, bias_rows, bias):
     pieces = 2 * C // P
-    bias_rows = keep.tile([P, P], BF16)
-    nc.vector.memset(bias_rows[:].bitcast(I32), 0)
-    nc.sync.dma_start(out=bias_rows[: pieces // 2, :], in_=bq.rearrange("(j k) -> j k", k=P))
-    nc.sync.dma_start(out=bias_rows[pieces // 2 : pieces, :], in_=bk.rearrange("(j k) -> j k", k=P))
     turned_rows = psum.tile([P, P], BF16, tag="turned")
     nc.tensor.transpose(turned_rows[:], bias_rows[:], identity[:])
     bias_columns = keep.tile([P, pieces], BF16)
@@ -49,43 +40,17 @@ def spread_biases(nc, keep, psum, identity, bq, bk):
     spread = psum.tile([P, pieces, P], BF16, tag="turned")
     for j in range(pieces):
         nc.tensor.transpose(spread[:, j, :], bias_columns[:, j : j + 1].to_broadcast([P, P]), identity[:])
-    bias = keep.tile([P, 2, C], BF16)
     nc.scalar.copy(out=bias[:].rearrange("p w (j k) -> p (w j) k", k=P), in_=spread[:])
-    return bias
 
 
-def pool_on_gpsimd(nc, work, x_chunk, sums):
-    rows = x_chunk[:, :, GPSIMD_FIRST:VECTOR_FIRST].rearrange("p t (a i w) -> p t a i w", i=2, w=W)
-    row_pairs = work.tile([P, PACK, 2 * GPSIMD_STRIPS, W], F32)
-    nc.gpsimd.tensor_tensor(out=row_pairs[:], in0=rows[:, :, :, 0, :], in1=rows[:, :, :, 1, :], op=ADD)
-    upper_lower = row_pairs[:].rearrange("p t (r h) w -> p (t r) h w", h=2)
-    columns = work.tile([P, PACK * GPSIMD_STRIPS, W], F32)
-    nc.gpsimd.tensor_tensor(
-        out=columns[:], in0=upper_lower[:, :, 0, :], in1=upper_lower[:, :, 1, :], op=ADD
-    )
-    pairs = columns[:].rearrange("p a (c e) -> p (a c) e", e=2)
-    column_pairs = work.tile([P, PACK * GPSIMD_STRIPS * W // 2], F32)
-    nc.gpsimd.tensor_tensor(out=column_pairs[:], in0=pairs[:, :, 0], in1=pairs[:, :, 1], op=ADD)
-    quads = column_pairs[:].rearrange("p (t n e) -> p t n e", t=PACK, e=2)
-    nc.gpsimd.tensor_tensor(
-        out=sums[:, TENSOR_BLOCKS:VECTOR_BLOCK, :].rearrange("p n t -> p t n"),
-        in0=quads[:, :, :, 0],
-        in1=quads[:, :, :, 1],
-        op=ADD,
-    )
-
-
-def pool_on_vector(nc, x_chunk, sums):
+def window_sums(nc, out, pixels):
     with nc.allow_low_precision(reason="added up in float32; the output is the one rounding to bfloat16"):
-        for t in range(PACK):
-            nc.vector.tensor_reduce(
-                out=sums[:, VECTOR_BLOCK:, t].rearrange("p (r c) -> p r c", c=BLOCK_COLS),
-                in_=x_chunk[:, t, VECTOR_FIRST:].rearrange(
-                    "p (r i c j) -> p r c i j", i=S, c=BLOCK_COLS, j=S
-                ),
-                axis=mybir.AxisListType.XY,
-                op=ADD,
-            )
+        nc.vector.tensor_reduce(
+            out=out.rearrange("p (r c) -> p r c", c=BLOCK_COLS),
+            in_=pixels.rearrange("p (r i c j) -> p r c i j", i=S, c=BLOCK_COLS, j=S),
+            axis=mybir.AxisListType.XY,
+            op=ADD,
+        )
 
 
 def tile_coarseblockattention_pa_kernel(
@@ -101,41 +66,44 @@ def tile_coarseblockattention_pa_kernel(
     ) as flipped, tc.tile_pool(name="results", bufs=N_CHUNKS) as results, tc.psum_pool(
         name="psum", bufs=2
     ) as psum, tc.manual_schedule():
-
-        def load_scales(w, scales):
-            for quadrant in range(4):
-                nc.sync.dma_start(
-                    out=w_scales[32 * quadrant : 32 * quadrant + 4, w, :].bitcast(I32),
-                    in_=scales[0, 4 * quadrant : 4 * quadrant + 4, :].bitcast(I32),
-                )
-
-        def load_pixels(c, first, last):
-            channels = x[c // CHUNKS].rearrange("(p t) h w -> p t (h w)", t=PACK)
-            start = (c % CHUNKS) * CHUNK
-            nc.sync.dma_start(out=x_chunks[c][:, :, first:last], in_=channels[:, :, start + first : start + last])
-
         identity = keep.tile([P, P], BF16)
         make_identity(nc, identity[:])
         word_identity = keep.tile([P, P], F32)
         make_identity(nc, word_identity[:])
+
         w_words = keep.tile([P, 2, 2 * C], U8, align_bytes=64)
         w_scales = keep.tile([P, 2, C], U8, align_bytes=64)
+        bias_rows = keep.tile([P, P], BF16)
+        bias = keep.tile([P, 2, C], BF16)
         nc.vector.memset(w_scales[:].rearrange("p w n -> p (w n)").bitcast(I32), 0)
-        x_chunks = [image.tile([P, PACK, CHUNK], BF16, name="x_chunk") for c in range(N_CHUNKS)]
+        nc.vector.memset(bias_rows[:].bitcast(I32), 0)
+        small_loads = [
+            (bias_rows[0:4, :], bq.rearrange("(j k) -> j k", k=P)),
+            (bias_rows[4:8, :], bk.rearrange("(j k) -> j k", k=P)),
+            (w_words[:, 0, :].bitcast(I32), Wq_words[0].bitcast(I32)),
+            (w_words[:, 1, :].bitcast(I32), Wk_words[0].bitcast(I32)),
+        ]
+        for w, scales in enumerate((Wq_scales, Wk_scales)):
+            for quadrant in range(4):
+                small_loads.append(
+                    (
+                        w_scales[32 * quadrant : 32 * quadrant + 4, w, :].bitcast(I32),
+                        scales[0, 4 * quadrant : 4 * quadrant + 4, :].bitcast(I32),
+                    )
+                )
 
-        bias = spread_biases(nc, keep, psum, identity, bq, bk)
-        load_scales(0, Wq_scales)
+        x_chunks = [image.tile([P, PACK, CHUNK], BF16, name="x_chunk") for c in range(N_CHUNKS)]
         for c in range(N_CHUNKS):
-            if c < SPLIT_CHUNKS:
-                load_pixels(c, GPSIMD_FIRST, VECTOR_FIRST)
-                load_pixels(c, VECTOR_FIRST, CHUNK)
-                load_pixels(c, 0, GPSIMD_FIRST)
-            else:
-                load_pixels(c, 0, CHUNK)
-            if c == 1:
-                load_scales(1, Wk_scales)
-                nc.sync.dma_start(out=w_words[:, 0, :].bitcast(I32), in_=Wq_words[0].bitcast(I32))
-                nc.sync.dma_start(out=w_words[:, 1, :].bitcast(I32), in_=Wk_words[0].bitcast(I32))
+            channels = x[c // CHUNKS].rearrange("(p t) h w -> p t (h w)", t=PACK)
+            offset = (c % CHUNKS) * CHUNK
+            for t in range(PACK):
+                nc.sync.dma_start(out=x_chunks[c][:, t, :], in_=channels[:, t, offset : offset + CHUNK])
+                riders = 2 * ((c - 1) * PACK + t)
+                if c > 0:
+                    for small_out, small_in in small_loads[riders : riders + 2]:
+                        nc.sync.dma_start(out=small_out, in_=small_in)
+
+        sums = [work.tile([P, PACK, P], BF16, name="sums", bufs=N_CHUNKS) for c in range(N_CHUNKS)]
 
         membership = keep.tile([P, BLOCK_COLS], F32)
         nc.vector.tensor_reduce(
@@ -149,19 +117,22 @@ def tile_coarseblockattention_pa_kernel(
         pixels = {}
 
         def turn(g):
-            turned = psum.tile([P, TENSOR_STRIPS, P], F32)
-            for k in range(TENSOR_STRIPS):
-                strip = x_chunks[g // PACK][:, g % PACK, k * STRIP : (k + 1) * STRIP]
+            strips = x_chunks[g // GROUPS_PER_CHUNK][:].rearrange("p t s -> p (t s)")
+            pixel = TENSOR_CHANNEL * CHUNK + (g % GROUPS_PER_CHUNK) * GROUP * STRIP
+            turned = psum.tile([P, GROUP, P], F32)
+            for k in range(GROUP):
+                strip = strips[:, pixel + k * STRIP : pixel + (k + 1) * STRIP]
                 nc.tensor.transpose(turned[:, k, :], strip.bitcast(F32), word_identity[:])
-            pixels[g] = flipped.tile([P, TENSOR_STRIPS, STRIP], BF16, name="pixels")
+            pixels[g] = flipped.tile([P, GROUP, STRIP], BF16, name="pixels")
             nc.scalar.copy(out=pixels[g][:], in_=turned[:].bitcast(BF16))
 
         def add_up(g, tensor_sums):
-            for k in range(TENSOR_STRIPS):
+            for k in range(GROUP):
                 even_odd = pixels[g][:, k, :].rearrange("q (p e) -> q p e", e=2)
+                block = ((g % GROUPS_PER_CHUNK) * GROUP + k) * BLOCK_COLS
                 for e in range(2):
                     nc.tensor.matmul(
-                        out=tensor_sums[:, g % PACK, k * BLOCK_COLS : (k + 1) * BLOCK_COLS],
+                        out=tensor_sums[:, block : block + BLOCK_COLS],
                         lhsT=even_odd[:, :, e],
                         rhs=block_of_word[:],
                         start=(e == 0),
@@ -169,33 +140,62 @@ def tile_coarseblockattention_pa_kernel(
                     )
 
         def pool_on_tensor(c):
-            tensor_sums = psum.tile([P, PACK, TENSOR_BLOCKS], F32)
-            for g in range(c * PACK, (c + 1) * PACK):
+            tensor_sums = psum.tile([P, TENSOR_STRIPS * BLOCK_COLS], F32)
+            for g in range(c * GROUPS_PER_CHUNK, (c + 1) * GROUPS_PER_CHUNK):
                 if g + AHEAD < GROUPS:
                     turn(g + AHEAD)
                 add_up(g, tensor_sums)
+            by_channel = sums[c][:].rearrange("p t n -> p (t n)")
             nc.scalar.copy(
-                out=sums[c][:, :TENSOR_BLOCKS, :], in_=tensor_sums[:].rearrange("p t n -> p n t")
+                out=by_channel[:, TENSOR_CHANNEL * P : TENSOR_CHANNEL * P + TENSOR_STRIPS * BLOCK_COLS],
+                in_=tensor_sums[:],
             )
 
-        sums, means, codes, accs, result = {}, {}, {}, {}, {}
+        def pool_on_vector(c):
+            window_sums(nc, sums[c][:, VECTOR_CHANNEL, :], x_chunks[c][:, VECTOR_CHANNEL, :])
+            window_sums(nc, sums[c][:, SHARED_CHANNEL, P // 2 :], x_chunks[c][:, SHARED_CHANNEL, HALF:])
 
-        def pool(c):
-            sums[c] = work.tile([P, P, PACK], BF16, name="sums")
-            pool_on_tensor(c)
-            pool_on_gpsimd(nc, work, x_chunks[c], sums[c])
-            pool_on_vector(nc, x_chunks[c], sums[c])
+        row_pairs, columns, column_pairs = {}, {}, {}
+
+        def add_row_pairs(c):
+            rows = x_chunks[c][:, GPSIMD_CHANNEL, :].rearrange("p (a i w) -> p a i w", i=2, w=W)
+            row_pairs[c] = work.tile([P, 2 * STRIPS, W], F32, name="row_pairs")
+            nc.gpsimd.tensor_tensor(out=row_pairs[c][:], in0=rows[:, :, 0, :], in1=rows[:, :, 1, :], op=ADD)
+
+        def add_rows(c):
+            upper_lower = row_pairs[c][:].rearrange("p (r h) w -> p r h w", h=2)
+            columns[c] = work.tile([P, STRIPS, W], F32, name="columns")
+            nc.gpsimd.tensor_tensor(
+                out=columns[c][:], in0=upper_lower[:, :, 0, :], in1=upper_lower[:, :, 1, :], op=ADD
+            )
+
+        def add_column_pairs(c):
+            pairs = columns[c][:].rearrange("p r (a e) -> p (r a) e", e=2)
+            column_pairs[c] = work.tile([P, STRIPS * W // 2], F32, name="column_pairs")
+            nc.gpsimd.tensor_tensor(out=column_pairs[c][:], in0=pairs[:, :, 0], in1=pairs[:, :, 1], op=ADD)
+
+        def add_columns(c):
+            quads = column_pairs[c][:].rearrange("p (n e) -> p n e", e=2)
+            nc.gpsimd.tensor_tensor(
+                out=sums[c][:, GPSIMD_CHANNEL, :], in0=quads[:, :, 0], in1=quads[:, :, 1], op=ADD
+            )
+
+        means, codes, accs, result = {}, {}, {}, {}
 
         def average(c):
-            means[c] = work.tile([P, P * PACK], BF16, name="means", align_bytes=64)
+            means[c] = work.tile([P, P, PACK], BF16, name="means", align_bytes=64)
             nc.vector.tensor_scalar_mul(
-                out=means[c][:], in0=sums[c][:].rearrange("p n t -> p (n t)"), scalar1=1.0 / (S * S)
+                out=means[c][:], in0=sums[c][:].rearrange("p t n -> p n t"), scalar1=1.0 / (S * S)
             )
 
         def quantise(c):
             x_codes = work.tile([P, P], U32, align_bytes=64)
             x_scales = work.tile([P, P], U8, align_bytes=64)
-            nc.vector.quantize_mx(out=x_codes[:].bitcast(FP8X4), scales=x_scales[:], in_=means[c][:])
+            nc.vector.quantize_mx(
+                out=x_codes[:].bitcast(FP8X4),
+                scales=x_scales[:],
+                in_=means[c][:].rearrange("p n t -> p (n t)"),
+            )
             codes[c] = (x_codes, x_scales)
 
         def multiply(c):
@@ -227,12 +227,21 @@ def tile_coarseblockattention_pa_kernel(
             if step >= 2:
                 multiply(step - 2)
             if step < N_CHUNKS:
-                pool(step)
+                pool_on_tensor(step)
+                pool_on_vector(step)
+                add_row_pairs(step)
+            if 1 <= step <= N_CHUNKS:
+                add_column_pairs(step - 1)
+            if step < N_CHUNKS:
+                add_rows(step)
+            if 1 <= step <= N_CHUNKS:
+                add_columns(step - 1)
+                average(step - 1)
+            if step == 1:
+                spread_biases(nc, keep, psum, identity, bias_rows, bias)
             if step >= 2:
                 finish(step - 2, 0)
             if 1 <= step <= N_CHUNKS:
-                average(step - 1)
+                quantise(step - 1)
             if step >= 2:
                 finish(step - 2, 1)
-            if 1 <= step <= N_CHUNKS:
-                quantise(step - 1)

@@ -20,12 +20,9 @@ CHUNK = STRIPS * STRIP
 CHUNKS = H * W // CHUNK
 N_CHUNKS = B * CHUNKS
 
-GPSIMD_CHANNEL, VECTOR_CHANNEL, TENSOR_CHANNEL, SHARED_CHANNEL = 0, 1, 2, 3
-HALF = CHUNK // 2
-TENSOR_STRIPS = STRIPS + STRIPS // 2
-GROUP = 4
-GROUPS_PER_CHUNK = TENSOR_STRIPS // GROUP
-GROUPS = N_CHUNKS * GROUPS_PER_CHUNK
+SHARES = [(2, 4, 2)] * 2 + [(2, 3, 3)] * 5 + [(0, 4, 4)]
+GROUPS = [(c, k) for c in range(N_CHUNKS) for k in range(SHARES[c][2])]
+STRIP_SUMS = PACK * BLOCK_COLS
 AHEAD = 2
 
 FLOPS = 2 * 2 * B * (H // S) * (W // S) * C * C
@@ -41,16 +38,6 @@ def spread_biases(nc, keep, psum, identity, bias_rows, bias):
     for j in range(pieces):
         nc.tensor.transpose(spread[:, j, :], bias_columns[:, j : j + 1].to_broadcast([P, P]), identity[:])
     nc.scalar.copy(out=bias[:].rearrange("p w (j k) -> p (w j) k", k=P), in_=spread[:])
-
-
-def window_sums(nc, out, pixels):
-    with nc.allow_low_precision(reason="added up in float32; the output is the one rounding to bfloat16"):
-        nc.vector.tensor_reduce(
-            out=out.rearrange("p (r c) -> p r c", c=BLOCK_COLS),
-            in_=pixels.rearrange("p (r i c j) -> p r c i j", i=S, c=BLOCK_COLS, j=S),
-            axis=mybir.AxisListType.XY,
-            op=ADD,
-        )
 
 
 def tile_coarseblockattention_pa_kernel(
@@ -103,7 +90,7 @@ def tile_coarseblockattention_pa_kernel(
                     for small_out, small_in in small_loads[riders : riders + 2]:
                         nc.sync.dma_start(out=small_out, in_=small_in)
 
-        sums = [work.tile([P, PACK, P], BF16, name="sums", bufs=N_CHUNKS) for c in range(N_CHUNKS)]
+        sums = [work.tile([P, PACK * P], BF16, name="sums", bufs=N_CHUNKS, align_bytes=64) for c in range(N_CHUNKS)]
 
         membership = keep.tile([P, BLOCK_COLS], F32)
         nc.vector.tensor_reduce(
@@ -117,19 +104,21 @@ def tile_coarseblockattention_pa_kernel(
         pixels = {}
 
         def turn(g):
-            strips = x_chunks[g // GROUPS_PER_CHUNK][:].rearrange("p t s -> p (t s)")
-            pixel = TENSOR_CHANNEL * CHUNK + (g % GROUPS_PER_CHUNK) * GROUP * STRIP
-            turned = psum.tile([P, GROUP, P], F32)
-            for k in range(GROUP):
-                strip = strips[:, pixel + k * STRIP : pixel + (k + 1) * STRIP]
+            c, group = GROUPS[g]
+            share = SHARES[c][2]
+            turned = psum.tile([P, PACK, P], F32)
+            for k in range(PACK):
+                t, r = divmod(group * PACK + k, share)
+                first_pixel = (STRIPS - share + r) * STRIP
+                strip = x_chunks[c][:, t, first_pixel : first_pixel + STRIP]
                 nc.tensor.transpose(turned[:, k, :], strip.bitcast(F32), word_identity[:])
-            pixels[g] = flipped.tile([P, GROUP, STRIP], BF16, name="pixels")
+            pixels[g] = flipped.tile([P, PACK, STRIP], BF16, name="pixels")
             nc.scalar.copy(out=pixels[g][:], in_=turned[:].bitcast(BF16))
 
         def add_up(g, tensor_sums):
-            for k in range(GROUP):
+            for k in range(PACK):
                 even_odd = pixels[g][:, k, :].rearrange("q (p e) -> q p e", e=2)
-                block = ((g % GROUPS_PER_CHUNK) * GROUP + k) * BLOCK_COLS
+                block = (GROUPS[g][1] * PACK + k) * BLOCK_COLS
                 for e in range(2):
                     nc.tensor.matmul(
                         out=tensor_sums[:, block : block + BLOCK_COLS],
@@ -140,53 +129,69 @@ def tile_coarseblockattention_pa_kernel(
                     )
 
         def pool_on_tensor(c):
-            tensor_sums = psum.tile([P, TENSOR_STRIPS * BLOCK_COLS], F32)
-            for g in range(c * GROUPS_PER_CHUNK, (c + 1) * GROUPS_PER_CHUNK):
-                if g + AHEAD < GROUPS:
-                    turn(g + AHEAD)
-                add_up(g, tensor_sums)
-            by_channel = sums[c][:].rearrange("p t n -> p (t n)")
+            share = SHARES[c][2]
+            tensor_sums = psum.tile([P, share * STRIP_SUMS], F32, name="tensor_sums")
+            for g, (chunk, group) in enumerate(GROUPS):
+                if chunk == c:
+                    if g + AHEAD < len(GROUPS):
+                        turn(g + AHEAD)
+                    add_up(g, tensor_sums)
             nc.scalar.copy(
-                out=by_channel[:, TENSOR_CHANNEL * P : TENSOR_CHANNEL * P + TENSOR_STRIPS * BLOCK_COLS],
-                in_=tensor_sums[:],
+                out=sums[c][:, (STRIPS - share) * STRIP_SUMS :].rearrange("p (r c t) -> p r c t", r=share, t=PACK),
+                in_=tensor_sums[:].rearrange("p (t r c) -> p r c t", r=share, t=PACK),
             )
 
         def pool_on_vector(c):
-            window_sums(nc, sums[c][:, VECTOR_CHANNEL, :], x_chunks[c][:, VECTOR_CHANNEL, :])
-            window_sums(nc, sums[c][:, SHARED_CHANNEL, P // 2 :], x_chunks[c][:, SHARED_CHANNEL, HALF:])
+            first, last = SHARES[c][0], SHARES[c][0] + SHARES[c][1]
+            blocks = sums[c][:, first * STRIP_SUMS : last * STRIP_SUMS].rearrange("p (n t) -> p n t", t=PACK)
+            for t in range(PACK):
+                with nc.allow_low_precision(reason="added up in float32; the output is the one rounding to bfloat16"):
+                    nc.vector.tensor_reduce(
+                        out=blocks[:, :, t].rearrange("p (r c) -> p r c", c=BLOCK_COLS),
+                        in_=x_chunks[c][:, t, first * STRIP : last * STRIP].rearrange(
+                            "p (r i c j) -> p r c i j", i=S, c=BLOCK_COLS, j=S
+                        ),
+                        axis=mybir.AxisListType.XY,
+                        op=ADD,
+                    )
 
         row_pairs, columns, column_pairs = {}, {}, {}
 
         def add_row_pairs(c):
-            rows = x_chunks[c][:, GPSIMD_CHANNEL, :].rearrange("p (a i w) -> p a i w", i=2, w=W)
-            row_pairs[c] = work.tile([P, 2 * STRIPS, W], F32, name="row_pairs")
-            nc.gpsimd.tensor_tensor(out=row_pairs[c][:], in0=rows[:, :, 0, :], in1=rows[:, :, 1, :], op=ADD)
+            share = SHARES[c][0]
+            rows = x_chunks[c][:, :, : share * STRIP].rearrange("p t (a i w) -> p t a i w", i=2, w=W)
+            row_pairs[c] = work.tile([P, PACK, 2 * share, W], F32, name="row_pairs")
+            step = 1 if c == 0 else PACK
+            for t in range(0, PACK, step):
+                nc.gpsimd.tensor_tensor(
+                    out=row_pairs[c][:, t : t + step],
+                    in0=rows[:, t : t + step, :, 0, :],
+                    in1=rows[:, t : t + step, :, 1, :],
+                    op=ADD,
+                )
 
         def add_rows(c):
-            upper_lower = row_pairs[c][:].rearrange("p (r h) w -> p r h w", h=2)
-            columns[c] = work.tile([P, STRIPS, W], F32, name="columns")
+            upper_lower = row_pairs[c][:].rearrange("p t (r h) w -> p (t r) h w", h=2)
+            columns[c] = work.tile([P, PACK * SHARES[c][0], W], F32, name="columns")
             nc.gpsimd.tensor_tensor(
                 out=columns[c][:], in0=upper_lower[:, :, 0, :], in1=upper_lower[:, :, 1, :], op=ADD
             )
 
         def add_column_pairs(c):
             pairs = columns[c][:].rearrange("p r (a e) -> p (r a) e", e=2)
-            column_pairs[c] = work.tile([P, STRIPS * W // 2], F32, name="column_pairs")
+            column_pairs[c] = work.tile([P, PACK * SHARES[c][0] * W // 2], F32, name="column_pairs")
             nc.gpsimd.tensor_tensor(out=column_pairs[c][:], in0=pairs[:, :, 0], in1=pairs[:, :, 1], op=ADD)
 
         def add_columns(c):
-            quads = column_pairs[c][:].rearrange("p (n e) -> p n e", e=2)
+            quads = column_pairs[c][:].rearrange("p (t n e) -> p n t e", t=PACK, e=2)
             nc.gpsimd.tensor_tensor(
-                out=sums[c][:, GPSIMD_CHANNEL, :], in0=quads[:, :, 0], in1=quads[:, :, 1], op=ADD
+                out=sums[c][:, : SHARES[c][0] * STRIP_SUMS].rearrange("p (n t) -> p n t", t=PACK),
+                in0=quads[:, :, :, 0],
+                in1=quads[:, :, :, 1],
+                op=ADD,
             )
 
-        means, codes, accs, result = {}, {}, {}, {}
-
-        def average(c):
-            means[c] = work.tile([P, P, PACK], BF16, name="means", align_bytes=64)
-            nc.vector.tensor_scalar_mul(
-                out=means[c][:], in0=sums[c][:].rearrange("p t n -> p n t"), scalar1=1.0 / (S * S)
-            )
+        codes, accs, result = {}, {}, {}
 
         def quantise(c):
             x_codes = work.tile([P, P], U32, align_bytes=64)
@@ -194,7 +199,7 @@ def tile_coarseblockattention_pa_kernel(
             nc.vector.quantize_mx(
                 out=x_codes[:].bitcast(FP8X4),
                 scales=x_scales[:],
-                in_=means[c][:].rearrange("p n t -> p (n t)"),
+                in_=sums[c][:],
             )
             codes[c] = (x_codes, x_scales)
 
@@ -216,32 +221,49 @@ def tile_coarseblockattention_pa_kernel(
             if w == 0:
                 result[c] = results.tile([P, 2, C], F32, name="result")
             first_block = (c % CHUNKS) * P
-            nc.vector.tensor_tensor(out=result[c][:, w, :], in0=accs[c, w][:], in1=bias[:, w, :], op=ADD)
+            nc.vector.scalar_tensor_tensor(
+                out=result[c][:, w, :],
+                in0=accs[c, w][:],
+                scalar=1.0 / (S * S),
+                in1=bias[:, w, :],
+                op0=mybir.AluOpType.mult,
+                op1=ADD,
+            )
             nc.sync.dma_start(
                 out=outs[w][c // CHUNKS, first_block : first_block + P, :], in_=result[c][:, w, :]
             )
 
         for g in range(AHEAD):
             turn(g)
-        for step in range(N_CHUNKS + 2):
-            if step >= 2:
-                multiply(step - 2)
-            if step < N_CHUNKS:
-                pool_on_tensor(step)
-                pool_on_vector(step)
+        last = N_CHUNKS - 1
+        for step in range(N_CHUNKS):
+            if step >= 3:
+                multiply(step - 3)
+            pool_on_tensor(step)
+            pool_on_vector(step)
+            if step < last:
                 add_row_pairs(step)
-            if 1 <= step <= N_CHUNKS:
+            if step >= 1:
                 add_column_pairs(step - 1)
-            if step < N_CHUNKS:
+            if step < last:
                 add_rows(step)
-            if 1 <= step <= N_CHUNKS:
+            if step >= 1:
                 add_columns(step - 1)
-                average(step - 1)
             if step == 1:
                 spread_biases(nc, keep, psum, identity, bias_rows, bias)
+            if step >= 3:
+                finish(step - 3, 0)
             if step >= 2:
-                finish(step - 2, 0)
-            if 1 <= step <= N_CHUNKS:
-                quantise(step - 1)
-            if step >= 2:
-                finish(step - 2, 1)
+                quantise(step - 2)
+            if step >= 3:
+                finish(step - 3, 1)
+        multiply(last - 2)
+        quantise(last - 1)
+        multiply(last - 1)
+        finish(last - 2, 0)
+        finish(last - 2, 1)
+        quantise(last)
+        multiply(last)
+        for c in (last - 1, last):
+            for w in range(2):
+                finish(c, w)

@@ -20,7 +20,7 @@ CHUNK = STRIPS * STRIP
 CHUNKS = H * W // CHUNK
 N_CHUNKS = B * CHUNKS
 
-SHARES = [(2, 4, 2)] * 2 + [(2, 3, 3)] * 5 + [(0, 4, 4)]
+SHARES = [(1, 5, 2), (2, 4, 2), (1, 4, 3)] + [(2, 3, 3)] * 4 + [(0, 4, 4)]
 GROUPS = [(c, k) for c in range(N_CHUNKS) for k in range(SHARES[c][2])]
 STRIP_SUMS = PACK * BLOCK_COLS
 AHEAD = 2
@@ -85,9 +85,9 @@ def tile_coarseblockattention_pa_kernel(
             offset = (c % CHUNKS) * CHUNK
             for t in range(PACK):
                 nc.sync.dma_start(out=x_chunks[c][:, t, :], in_=channels[:, t, offset : offset + CHUNK])
-                riders = 2 * ((c - 1) * PACK + t)
+                riders = (c - 1) * PACK + t
                 if c > 0:
-                    for small_out, small_in in small_loads[riders : riders + 2]:
+                    for small_out, small_in in small_loads[riders : riders + 1]:
                         nc.sync.dma_start(out=small_out, in_=small_in)
 
         sums = [work.tile([P, PACK * P], BF16, name="sums", bufs=N_CHUNKS, align_bytes=64) for c in range(N_CHUNKS)]

@@ -83,11 +83,12 @@ def tile_coarseblockattention_pa_kernel(
         for c in range(N_CHUNKS):
             channels = x[c // CHUNKS].rearrange("(p t) h w -> p t (h w)", t=PACK)
             offset = (c % CHUNKS) * CHUNK
-            for t in range(PACK):
-                nc.sync.dma_start(out=x_chunks[c][:, t, :], in_=channels[:, t, offset : offset + CHUNK])
+            n = 2 if c > 0 else 1
+            for t in range(0, PACK, n):
+                nc.sync.dma_start(out=x_chunks[c][:, t : t + n, :], in_=channels[:, t : t + n, offset : offset + CHUNK])
                 riders = (c - 1) * PACK + t
                 if c > 0:
-                    for small_out, small_in in small_loads[riders : riders + 1]:
+                    for small_out, small_in in small_loads[riders : riders + n]:
                         nc.sync.dma_start(out=small_out, in_=small_in)
 
         sums = [work.tile([P, PACK * P], BF16, name="sums", bufs=N_CHUNKS, align_bytes=64) for c in range(N_CHUNKS)]

import concourse.mybir as mybir
from concourse.masks import make_identity

BF16 = mybir.dt.bfloat16
F32 = mybir.dt.float32
I32 = mybir.dt.int32
U8 = mybir.dt.uint8
U32 = mybir.dt.uint32
FP8X4 = mybir.dt.float8_e4m3fn_x4
FP4X4 = mybir.dt.float4_e2m1fn_x4
ADD = mybir.AluOpType.add

B, C, H, W, S = 2, 512, 128, 64, 4
P = 128
PACK = 4
BLOCK_COLS = W // S
STRIP = S * W
STRIPS = P // BLOCK_COLS
CHUNK = STRIPS * STRIP
CHUNKS = H * W // CHUNK
N_CHUNKS = B * CHUNKS

SHARES = [(1, 5, 2), (2, 4, 2), (1, 4, 3)] + [(2, 3, 3)] * 4 + [(0, 4, 4)]
GROUPS = [(c, k) for c in range(N_CHUNKS) for k in range(SHARES[c][2])]
STRIP_SUMS = PACK * BLOCK_COLS
AHEAD = 2

FLOPS = 2 * 2 * B * (H // S) * (W // S) * C * C


def spread_biases(nc, keep, psum, identity, bias_rows, bias):
    pieces = 2 * C // P
    turned_rows = psum.tile([P, P], BF16, tag="turned")
    nc.tensor.transpose(turned_rows[:], bias_rows[:], identity[:])
    bias_columns = keep.tile([P, pieces], BF16)
    nc.scalar.copy(out=bias_columns[:], in_=turned_rows[:, :pieces])
    spread = psum.tile([P, pieces, P], BF16, tag="turned")
    for j in range(pieces):
        nc.tensor.transpose(spread[:, j, :], bias_columns[:, j : j + 1].to_broadcast([P, P]), identity[:])
    nc.scalar.copy(out=bias[:].rearrange("p w (j k) -> p (w j) k", k=P), in_=spread[:])


def tile_coarseblockattention_pa_kernel(
    tc, x, Wq_words, Wq_scales, bq, Wk_words, Wk_scales, bk, out_0, out_1
):
    nc = tc.nc
    outs = (out_0, out_1)

    with tc.tile_pool(name="keep", bufs=1) as keep, tc.tile_pool(
        name="image", bufs=N_CHUNKS
    ) as image, tc.tile_pool(name="work", bufs=3) as work, tc.tile_pool(
        name="flipped", bufs=AHEAD + 2
    ) as flipped, tc.tile_pool(name="results", bufs=N_CHUNKS) as results, tc.psum_pool(
        name="psum", bufs=2
    ) as psum, tc.manual_schedule():
        identity = keep.tile([P, P], BF16)
        make_identity(nc, identity[:])
        word_identity = keep.tile([P, P], F32)
        make_identity(nc, word_identity[:])

        w_words = keep.tile([P, 2, 2 * C], U8, align_bytes=64)
        w_scales = keep.tile([P, 2, C], U8, align_bytes=64)
        bias_rows = keep.tile([P, P], BF16)
        bias = keep.tile([P, 2, C], BF16)
        nc.vector.memset(w_scales[:].rearrange("p w n -> p (w n)").bitcast(I32), 0)
        nc.vector.memset(bias_rows[:].bitcast(I32), 0)
        small_loads = [
            (bias_rows[0:4, :], bq.rearrange("(j k) -> j k", k=P)),
            (bias_rows[4:8, :], bk.rearrange("(j k) -> j k", k=P)),
            (w_words[:, 0, :].bitcast(I32), Wq_words[0].bitcast(I32)),
            (w_words[:, 1, :].bitcast(I32), Wk_words[0].bitcast(I32)),
        ]
        for w, scales in enumerate((Wq_scales, Wk_scales)):
            for quadrant in range(4):
                small_loads.append(
                    (
                        w_scales[32 * quadrant : 32 * quadrant + 4, w, :].bitcast(I32),
                        scales[0, 4 * quadrant : 4 * quadrant + 4, :].bitcast(I32),
                    )
                )

        x_chunks = [image.tile([P, PACK, CHUNK], BF16, name="x_chunk") for c in range(N_CHUNKS)]
        for c in range(N_CHUNKS):
            channels = x[c // CHUNKS].rearrange("(p t) h w -> p t (h w)", t=PACK)
            offset = (c % CHUNKS) * CHUNK
            n = 2 if c > 0 else 1
            for t in range(0, PACK, n):
                nc.sync.dma_start(out=x_chunks[c][:, t : t + n, :], in_=channels[:, t : t + n, offset : offset + CHUNK])
                riders = (c - 1) * PACK + t
                if c > 0:
                    for small_out, small_in in small_loads[riders : riders + n]:
                        nc.sync.dma_start(out=small_out, in_=small_in)

        sums = [work.tile([P, PACK * P], BF16, name="sums", bufs=N_CHUNKS, align_bytes=64) for c in range(N_CHUNKS)]

        membership = keep.tile([P, BLOCK_COLS], F32)
        nc.vector.tensor_reduce(
            out=membership[:],
            in_=identity[:].rearrange("p (i c j) -> p c i j", i=S, c=BLOCK_COLS, j=S // 2),
            axis=mybir.AxisListType.XY,
            op=ADD,
        )
        block_of_word = keep.tile([P, BLOCK_COLS], BF16)
        nc.vector.tensor_copy(out=block_of_word[:], in_=membership[:])
        pixels = {}

        def turn(g):
            c, group = GROUPS[g]
            share = SHARES[c][2]
            turned = psum.tile([P, PACK, P], F32)
            for k in range(PACK):
                t, r = divmod(group * PACK + k, share)
                first_pixel = (STRIPS - share + r) * STRIP
                strip = x_chunks[c][:, t, first_pixel : first_pixel + STRIP]
                nc.tensor.transpose(turned[:, k, :], strip.bitcast(F32), word_identity[:])
            pixels[g] = flipped.tile([P, PACK, STRIP], BF16, name="pixels")
            nc.scalar.copy(out=pixels[g][:], in_=turned[:].bitcast(BF16))

        def add_up(g, tensor_sums):
            for k in range(PACK):
                even_odd = pixels[g][:, k, :].rearrange("q (p e) -> q p e", e=2)
                block = (GROUPS[g][1] * PACK + k) * BLOCK_COLS
                for e in range(2):
                    nc.tensor.matmul(
                        out=tensor_sums[:, block : block + BLOCK_COLS],
                        lhsT=even_odd[:, :, e],
                        rhs=block_of_word[:],
                        start=(e == 0),
                        stop=(e == 1),
                    )

        def pool_on_tensor(c):
            share = SHARES[c][2]
            tensor_sums = psum.tile([P, share * STRIP_SUMS], F32, name="tensor_sums")
            for g, (chunk, group) in enumerate(GROUPS):
                if chunk == c:
                    if g + AHEAD < len(GROUPS):
                        turn(g + AHEAD)
                    add_up(g, tensor_sums)
            nc.scalar.copy(
                out=sums[c][:, (STRIPS - share) * STRIP_SUMS :].rearrange("p (r c t) -> p r c t", r=share, t=PACK),
                in_=tensor_sums[:].rearrange("p (t r c) -> p r c t", r=share, t=PACK),
            )

        def pool_on_vector(c):
            first, last = SHARES[c][0], SHARES[c][0] + SHARES[c][1]
            blocks = sums[c][:, first * STRIP_SUMS : last * STRIP_SUMS].rearrange("p (n t) -> p n t", t=PACK)
            for t in range(PACK):
                with nc.allow_low_precision(reason="added up in float32; the output is the one rounding to bfloat16"):
                    nc.vector.tensor_reduce(
                        out=blocks[:, :, t].rearrange("p (r c) -> p r c", c=BLOCK_COLS),
                        in_=x_chunks[c][:, t, first * STRIP : last * STRIP].rearrange(
                            "p (r i c j) -> p r c i j", i=S, c=BLOCK_COLS, j=S
                        ),
                        axis=mybir.AxisListType.XY,
                        op=ADD,
                    )

        row_pairs, columns, column_pairs = {}, {}, {}

        def add_row_pairs(c):
            share = SHARES[c][0]
            rows = x_chunks[c][:, :, : share * STRIP].rearrange("p t (a i w) -> p t a i w", i=2, w=W)
            row_pairs[c] = work.tile([P, PACK, 2 * share, W], F32, name="row_pairs")
            step = 1 if c == 0 else PACK
            for t in range(0, PACK, step):
                nc.gpsimd.tensor_tensor(
                    out=row_pairs[c][:, t : t + step],
                    in0=rows[:, t : t + step, :, 0, :],
                    in1=rows[:, t : t + step, :, 1, :],
                    op=ADD,
                )

        def add_rows(c):
            upper_lower = row_pairs[c][:].rearrange("p t (r h) w -> p (t r) h w", h=2)
            columns[c] = work.tile([P, PACK * SHARES[c][0], W], F32, name="columns")
            nc.gpsimd.tensor_tensor(
                out=columns[c][:], in0=upper_lower[:, :, 0, :], in1=upper_lower[:, :, 1, :], op=ADD
            )

        def add_column_pairs(c):
            pairs = columns[c][:].rearrange("p r (a e) -> p (r a) e", e=2)
            column_pairs[c] = work.tile([P, PACK * SHARES[c][0] * W // 2], F32, name="column_pairs")
            nc.gpsimd.tensor_tensor(out=column_pairs[c][:], in0=pairs[:, :, 0], in1=pairs[:, :, 1], op=ADD)

        def add_columns(c):
            quads = column_pairs[c][:].rearrange("p (t n e) -> p n t e", t=PACK, e=2)
            nc.gpsimd.tensor_tensor(
                out=sums[c][:, : SHARES[c][0] * STRIP_SUMS].rearrange("p (n t) -> p n t", t=PACK),
                in0=quads[:, :, :, 0],
                in1=quads[:, :, :, 1],
                op=ADD,
            )

        codes, accs, result = {}, {}, {}

        def quantise(c):
            x_codes = work.tile([P, P], U32, align_bytes=64)
            x_scales = work.tile([P, P], U8, align_bytes=64)
            nc.vector.quantize_mx(
                out=x_codes[:].bitcast(FP8X4),
                scales=x_scales[:],
                in_=sums[c][:],
            )
            codes[c] = (x_codes, x_scales)

        def multiply(c):
            x_codes, x_scales = codes[c]
            for w in range(2):
                accs[c, w] = psum.tile([P, C], F32, name="acc%d" % w)
                nc.tensor.matmul_mx(
                    out=accs[c, w][:],
                    lhsT=x_codes[:].bitcast(FP8X4),
                    lhsT_scale=x_scales[:],
                    rhs=w_words[:, w, :].bitcast(FP4X4),
                    rhs_scale=w_scales[:, w, :],
                    start=True,
                    stop=True,
                )

        def finish(c, w):
            if w == 0:
                result[c] = results.tile([P, 2, C], F32, name="result")
            first_block = (c % CHUNKS) * P
            nc.vector.scalar_tensor_tensor(
                out=result[c][:, w, :],
                in0=accs[c, w][:],
                scalar=1.0 / (S * S),
                in1=bias[:, w, :],
                op0=mybir.AluOpType.mult,
                op1=ADD,
            )
            nc.sync.dma_start(
                out=outs[w][c // CHUNKS, first_block : first_block + P, :], in_=result[c][:, w, :]
            )

        for g in range(AHEAD):
            turn(g)
        last = N_CHUNKS - 1
        for step in range(N_CHUNKS):
            if step >= 3:
                multiply(step - 3)
            pool_on_tensor(step)
            pool_on_vector(step)
            if step < last:
                add_row_pairs(step)
            if step >= 1:
                add_column_pairs(step - 1)
            if step < last:
                add_rows(step)
            if step >= 1:
                add_columns(step - 1)
            if step == 1:
                spread_biases(nc, keep, psum, identity, bias_rows, bias)
            if step >= 3:
                finish(step - 3, 0)
            if step >= 2:
                quantise(step - 2)
            if step >= 3:
                finish(step - 3, 1)
        multiply(last - 2)
        quantise(last - 1)
        multiply(last - 1)
        finish(last - 2, 0)
        finish(last - 2, 1)
        quantise(last)
        multiply(last)
        for c in (last - 1, last):
            for w in range(2):
                finish(c, w)
